import numpy as np
import ml_dtypes


def mxq(x, axis, fmt="e4m3"):
    dtype, down = {"e4m3": (ml_dtypes.float8_e4m3fn, 7), "e5m2": (ml_dtypes.float8_e5m2, 14)}[fmt]
    v = np.moveaxis(np.asarray(x, np.float32).astype(ml_dtypes.bfloat16).astype(np.float64), axis, -1)
    blocks = v.reshape(v.shape[:-1] + (-1, 32))
    amax = np.abs(blocks).max(-1, keepdims=True)
    byte = np.maximum(np.where(amax > 0, np.frexp(amax)[1] - 1 + 127, 0) - down, 1)
    scale = np.exp2(byte - 127.0)
    codes = (blocks / scale).astype(np.float32).astype(dtype).astype(np.float64)
    return np.moveaxis((codes * scale).reshape(v.shape), -1, axis)


WIDE = False


def mx_kscale(k):
    if not WIDE:
        return np.ones(k)
    levels = np.array([10, -10, 5, -5, 0])
    if k % 512:
        return np.exp2(np.random.permutation(np.resize(levels, k // 32))).repeat(32)
    a = np.empty((k // 512, 16))
    for p in range(k // 512):
        a[p, :8] = np.random.permutation(np.resize(levels, 8))
        for g in range(8):
            far = levels[np.abs(levels - a[p, g]) >= 10]
            a[p, g + 8] = far[np.random.randint(len(far))]
    return np.exp2(a.ravel()).repeat(32)


BF16 = ml_dtypes.bfloat16


def bf(x):
    return np.asarray(x, np.float32).astype(BF16)


def f64(x):
    return np.asarray(x).astype(np.float64)


B, N, D, R, Q = 4, 4096, 512, 8, 16


def setup_inputs():
    s = mx_kscale(D)
    return {"x": bf(np.random.standard_normal((B, N, D)) * s),
            "w0": bf(np.random.standard_normal((B, N, R))),
            "core1": bf(np.random.standard_normal((R, D, Q)) / np.sqrt(D * R) / s[None, :, None]),
            "core2": bf(np.random.standard_normal((Q, D, R)) / np.sqrt(D * Q) / s[None, :, None])}


def reference(x, w0, core1, core2):
    xq = mxq(f64(x), 2, "e4m3")
    c1 = mxq(f64(core1), 1, "e4m3").transpose(1, 0, 2).reshape(D, R * Q)
    c2 = mxq(f64(core2), 1, "e4m3").transpose(1, 0, 2).reshape(D, Q * R)
    m1 = (xq @ c1).reshape(B, N, R, Q)
    m2 = (xq @ c2).reshape(B, N, Q, R)
    w1 = (f64(w0)[..., :, None] * m1).sum(-2)
    w2 = (w1[..., :, None] * m2).sum(-2)
    return w2

@@ -1,0 +1,244 @@
+from contextlib import ExitStack
+
+import concourse.mybir as mybir
+from concourse.masks import make_identity
+
+F32 = mybir.dt.float32
+BF16 = mybir.dt.bfloat16
+U32 = mybir.dt.uint32
+U8 = mybir.dt.uint8
+FP8X4 = mybir.dt.float8_e4m3fn_x4
+MULT = mybir.AluOpType.mult
+ADD = mybir.AluOpType.add
+
+P = 128
+TOKENS = 4 * 4096
+D = 512
+R = 8
+Q = 16
+TILES = TOKENS // P
+QUAD = 4
+NQ = TILES // QUAD
+OCT = 8
+NB = TILES // OCT
+BATCH = 16
+NO = TILES // BATCH
+
+FLOPS = 2 * TOKENS * D * (R * Q + Q * R) + 2 * TOKENS * (R * Q + Q * R)
+
+
+def tile_linear_pa_t_kernel(tc, x, w0, core1, core2, out):
+    nc = tc.nc
+    xv = x.flatten_outer_dims().rearrange("(p t) d -> p t d", t=TILES)
+    w0v = w0.flatten_outer_dims().rearrange("(p t) r -> p t r", t=TILES)
+    ov = out.flatten_outer_dims().rearrange("(p t) r -> p t r", t=TILES)
+
+    with ExitStack() as ctx:
+        const = ctx.enter_context(tc.tile_pool(name="const", bufs=1))
+        xin = ctx.enter_context(tc.tile_pool(name="xin", bufs=1))
+        gp = ctx.enter_context(tc.tile_pool(name="gp", bufs=3))
+        cp = ctx.enter_context(tc.tile_pool(name="cp", bufs=5))
+        p1p = ctx.enter_context(tc.tile_pool(name="p1p", bufs=4))
+        ep = ctx.enter_context(tc.tile_pool(name="ep", bufs=2))
+        h2p = ctx.enter_context(tc.tile_pool(name="h2p", bufs=1))
+        xtp = ctx.enter_context(tc.psum_pool(name="xtp", bufs=3))
+        m1p = ctx.enter_context(tc.psum_pool(name="m1p", bufs=2))
+        m2p = ctx.enter_context(tc.psum_pool(name="m2p", bufs=2))
+        op = ctx.enter_context(tc.psum_pool(name="op", bufs=1))
+        ctx.enter_context(tc.manual_schedule())
+
+        c1raw = const.tile([P, R, 4 * Q], BF16, name="c1raw")
+        c2raw = const.tile([P, Q, 4 * R], BF16, name="c2raw")
+        nc.scalar.dma_start(out=c1raw[:], in_=core1.rearrange("r (p e) q -> p r (e q)", e=4))
+        nc.scalar.dma_start(out=c2raw[:], in_=core2.rearrange("q (p e) r -> p q (e r)", e=4))
+        w0_sb = const.tile([P, TILES, R], BF16, name="w0_sb")
+        nc.scalar.dma_start(out=w0_sb[:], in_=w0v)
+        xq = []
+        for i in range(NQ):
+            xt_in = xin.tile([P, QUAD, D], BF16, name="x%d" % i)
+            nc.sync.dma_start(out=xt_in[:], in_=xv[:, QUAD * i : QUAD * i + QUAD, :])
+            xq.append(xt_in)
+
+        ident = const.tile([P, P], F32, name="ident")
+        make_identity(nc, ident[:])
+
+        cg = const.tile([P, 2 * P, 4], BF16, name="cg", align_bytes=64)
+        nc.vector.tensor_copy(
+            out=cg[:, 0:P, :].rearrange("p (r q) e -> p r q e", q=Q),
+            in_=c1raw[:].rearrange("p r (e q) -> p r q e", e=4),
+        )
+        nc.vector.tensor_copy(
+            out=cg[:, P : 2 * P, :].rearrange("p (q r) e -> p q r e", r=R),
+            in_=c2raw[:].rearrange("p q (e r) -> p q r e", e=4),
+        )
+        cc = const.tile([P, 2 * P], U32, name="cc", align_bytes=64)
+        cs = const.tile([P, 2 * P], U8, name="cs", align_bytes=64)
+        nc.vector.quantize_mx(
+            out=cc[:].bitcast(FP8X4), scales=cs[:], in_=cg[:].rearrange("p c t -> p (c t)")
+        )
+
+        out_sb = const.tile([P, TILES, R], F32, name="out_sb")
+
+        gs = {}
+        cods = {}
+        m1s = {}
+        m2s = {}
+        p1s = {}
+        h1s = {}
+        h2s = {}
+        w1s = {}
+        p2s = {}
+        obank = {}
+        oTss = {}
+
+        def transpose_pair(j, h):
+            if h == 0:
+                gs[j] = gp.tile([P, OCT, P, 4], BF16, name="g", tag="g", align_bytes=64)
+            x32 = xq[2 * j + h // 2][:].bitcast(F32)
+            xt = xtp.tile([P, 2, 2, P], F32, name="xt", tag="xt")
+            for a in range(2):
+                for u in range(2):
+                    nc.tensor.transpose(
+                        xt[:, a, u, :], x32[:, 2 * (h % 2) + a, u : 2 * P : 2], ident[:]
+                    )
+            nc.scalar.copy(
+                out=gs[j][:].bitcast(F32)[:, 2 * h : 2 * h + 2, :, :],
+                in_=xt[:].rearrange("p a u k -> p a k u"),
+            )
+
+        def quantise(j):
+            cod = cp.tile([P, OCT * P], U32, name="cod", tag="cod", align_bytes=64)
+            scl = cp.tile([P, OCT * P], U8, name="scl", tag="scl", align_bytes=64)
+            nc.vector.quantize_mx(
+                out=cod[:].bitcast(FP8X4),
+                scales=scl[:],
+                in_=gs[j][:].rearrange("p a k t -> p (a k t)"),
+            )
+            cods[j] = (cod, scl)
+
+        def mx_quad(k, half, pool, store):
+            cod, scl = cods[k // 2]
+            m = pool.tile([P, QUAD, P], F32, name="m%d" % half, tag="m%d" % half)
+            for a in range(QUAD):
+                c0 = (QUAD * (k % 2) + a) * P
+                nc.tensor.matmul_mx(
+                    out=m[:, a, :],
+                    lhsT=cod[:, c0 : c0 + P].bitcast(FP8X4),
+                    lhsT_scale=scl[:, c0 : c0 + P],
+                    rhs=cc[:, half * P : (half + 1) * P].bitcast(FP8X4),
+                    rhs_scale=cs[:, half * P : (half + 1) * P],
+                    start=True,
+                    stop=True,
+                )
+            store[k] = m
+
+        def stage1_mul(k):
+            p1 = p1p.tile([P, R, QUAD, Q], F32, name="p1", tag="p1")
+            nc.vector.tensor_tensor(
+                out=p1[:].rearrange("p r a q -> p a r q"),
+                in0=m1s[k][:].rearrange("p a (r q) -> p a r q", q=Q),
+                in1=w0_sb[:, QUAD * k : QUAD * k + QUAD, :].unsqueeze(3).to_broadcast([P, QUAD, R, Q]),
+                op=MULT,
+            )
+            p1s[k] = p1
+
+        def stage1_fold8to4(k):
+            j, h = divmod(k, 2)
+            if h == 0:
+                h1s[j] = ep.tile([P, 2, 4, QUAD * Q], F32, name="h1", tag="h1")
+            nc.gpsimd.tensor_tensor(
+                out=h1s[j][:, h, :, :].rearrange("p r c -> p (r c)"),
+                in0=p1s[k][:, 0:4, :, :].rearrange("p r a q -> p (r a q)"),
+                in1=p1s[k][:, 4:8, :, :].rearrange("p r a q -> p (r a q)"),
+                op=ADD,
+            )
+
+        def stage1_fold4to2(j):
+            h2 = h2p.tile([P, 2, 2, QUAD * Q], F32, name="h2", tag="h2")
+            nc.gpsimd.tensor_tensor(
+                out=h2[:].rearrange("p h r c -> p h (r c)"),
+                in0=h1s[j][:, :, 0:2, :].rearrange("p h r c -> p h (r c)"),
+                in1=h1s[j][:, :, 2:4, :].rearrange("p h r c -> p h (r c)"),
+                op=ADD,
+            )
+            h2s[j] = h2
+
+        def stage1_fold2to1(j):
+            w1 = ep.tile([P, 2, QUAD * Q], F32, name="w1", tag="w1")
+            nc.vector.tensor_tensor(
+                out=w1[:], in0=h2s[j][:, :, 0, :], in1=h2s[j][:, :, 1, :], op=ADD
+            )
+            w1s[j] = w1
+
+        def stage2_mul(k):
+            b, i = divmod(k, BATCH // QUAD)
+            if i == 0:
+                p2s[b] = ep.tile([P, Q, BATCH, R], F32, name="p2", tag="p2")
+            nc.vector.tensor_tensor(
+                out=p2s[b][:, :, QUAD * i : QUAD * i + QUAD, :].rearrange("p q a r -> p a q r"),
+                in0=m2s[k][:].rearrange("p a (q r) -> p a q r", r=R),
+                in1=w1s[k // 2][:, k % 2, :]
+                .rearrange("p (a q) -> p a q", q=Q)
+                .unsqueeze(3)
+                .to_broadcast([P, QUAD, Q, R]),
+                op=MULT,
+            )
+
+        def sum_batch(b, q0, q1):
+            if q0 == 0:
+                obank[b] = op.tile([P, 2, P], F32, name="o", tag="o")
+            o = obank[b]
+            for q in range(q0, q1):
+                nc.tensor.matmul(
+                    out=o[:, 0, :],
+                    lhsT=p2s[b][:, q, :, :].rearrange("p a r -> p (a r)"),
+                    rhs=ident[:],
+                    start=(q == 0),
+                    stop=(q == Q - 1),
+                    is_transpose=True,
+                )
+            if q1 == Q:
+                oTs = ep.tile([P, P], F32, name="oTs", tag="oTs")
+                nc.scalar.copy(out=oTs[:], in_=o[:, 0, :])
+                oTss[b] = oTs
+
+        def finish_batch(b):
+            o = obank[b]
+            nc.tensor.transpose(o[:, 1, :], oTss[b][:], ident[:])
+            dst = out_sb[:, BATCH * b : BATCH * b + BATCH, :]
+            nc.scalar.copy(out=dst.rearrange("p a r -> p (a r)"), in_=o[:, 1, :])
+            nc.sync.dma_start(out=ov[:, BATCH * b : BATCH * b + BATCH, :], in_=dst)
+
+        def inside(j):
+            return 0 <= j < NB
+
+        for s in range(-3, NB + 7):
+            if inside(s - 2):
+                stage1_fold2to1(s - 2)
+            if inside(s - 1):
+                stage1_fold4to2(s - 1)
+            if inside(s - 6) and (s - 6) % 2 == 0:
+                finish_batch((s - 6) // 2)
+            if inside(s + 3):
+                for h in range(3):
+                    transpose_pair(s + 3, h)
+            if inside(s - 4):
+                b, part = divmod(s - 4, 2)
+                sum_batch(b, part * (Q // 2), (part + 1) * (Q // 2))
+            if inside(s + 3):
+                transpose_pair(s + 3, 3)
+            if inside(s):
+                for k in (2 * s, 2 * s + 1):
+                    stage1_mul(k)
+                    stage1_fold8to4(k)
+            if inside(s - 2):
+                for k in (2 * s - 4, 2 * s - 3):
+                    stage2_mul(k)
+            if inside(s + 1):
+                for k in (2 * s + 2, 2 * s + 3):
+                    mx_quad(k, 0, m1p, m1s)
+            if inside(s - 1):
+                for k in (2 * s - 2, 2 * s - 1):
+                    mx_quad(k, 1, m2p, m2s)
+            if inside(s + 2):
+                quantise(s + 2)

@@ -23,6 +23,7 @@ OCT = 8
 NB = TILES // OCT
 BATCH = 16
 NO = TILES // BATCH
+FIRST_REGROUPED = 4
 
 FLOPS = 2 * TOKENS * D * (R * Q + Q * R) + 2 * TOKENS * (R * Q + Q * R)
 
@@ -37,6 +38,7 @@ def tile_linear_pa_t_kernel(tc, x, w0, core1, core2, out):
         const = ctx.enter_context(tc.tile_pool(name="const", bufs=1))
         xin = ctx.enter_context(tc.tile_pool(name="xin", bufs=1))
         gp = ctx.enter_context(tc.tile_pool(name="gp", bufs=3))
+        xpp = ctx.enter_context(tc.tile_pool(name="xpp", bufs=4))
         cp = ctx.enter_context(tc.tile_pool(name="cp", bufs=5))
         p1p = ctx.enter_context(tc.tile_pool(name="p1p", bufs=4))
         ep = ctx.enter_context(tc.tile_pool(name="ep", bufs=2))
@@ -80,6 +82,7 @@ def tile_linear_pa_t_kernel(tc, x, w0, core1, core2, out):
         out_sb = const.tile([P, TILES, R], F32, name="out_sb")
 
         gs = {}
+        xps = {}
         cods = {}
         m1s = {}
         m2s = {}
@@ -91,6 +94,12 @@ def tile_linear_pa_t_kernel(tc, x, w0, core1, core2, out):
         obank = {}
         oTss = {}
 
+        def regroup_quad(i):
+            xp = xpp.tile([P, 2, 2, P], F32, name="xp", tag="xp")
+            x32 = xq[i][:].bitcast(F32)
+            nc.scalar.copy(out=xp[:], in_=x32[:, 0:QUAD:2, :].rearrange("p a (k u) -> p a u k", u=2))
+            xps[i] = xp
+
         def transpose_pair(j, h):
             if h == 0:
                 gs[j] = gp.tile([P, OCT, P, 4], BF16, name="g", tag="g", align_bytes=64)
@@ -98,9 +107,11 @@ def tile_linear_pa_t_kernel(tc, x, w0, core1, core2, out):
             xt = xtp.tile([P, 2, 2, P], F32, name="xt", tag="xt")
             for a in range(2):
                 for u in range(2):
-                    nc.tensor.transpose(
-                        xt[:, a, u, :], x32[:, 2 * (h % 2) + a, u : 2 * P : 2], ident[:]
-                    )
+                    if a == 0 and j >= FIRST_REGROUPED:
+                        src = xps[2 * j + h // 2][:, h % 2, u, :]
+                    else:
+                        src = x32[:, 2 * (h % 2) + a, u : 2 * P : 2]
+                    nc.tensor.transpose(xt[:, a, u, :], src, ident[:])
             nc.scalar.copy(
                 out=gs[j][:].bitcast(F32)[:, 2 * h : 2 * h + 2, :, :],
                 in_=xt[:].rearrange("p a u k -> p a k u"),
@@ -222,6 +233,8 @@ def tile_linear_pa_t_kernel(tc, x, w0, core1, core2, out):
             if inside(s + 3):
                 for h in range(3):
                     transpose_pair(s + 3, h)
+                    if h < 2 and FIRST_REGROUPED <= s + 4 < NB:
+                        regroup_quad(2 * (s + 4) + h)
             if inside(s - 4):
                 b, part = divmod(s - 4, 2)
                 sum_batch(b, part * (Q // 2), (part + 1) * (Q // 2))

@@ -41,8 +41,9 @@ def tile_linear_pa_t_kernel(tc, x, w0, core1, core2, out):
         xpp = ctx.enter_context(tc.tile_pool(name="xpp", bufs=4))
         cp = ctx.enter_context(tc.tile_pool(name="cp", bufs=5))
         p1p = ctx.enter_context(tc.tile_pool(name="p1p", bufs=4))
-        ep = ctx.enter_context(tc.tile_pool(name="ep", bufs=2))
-        h2p = ctx.enter_context(tc.tile_pool(name="h2p", bufs=1))
+        ep = ctx.enter_context(tc.tile_pool(name="ep", bufs=3))
+        p2p = ctx.enter_context(tc.tile_pool(name="p2p", bufs=2))
+        h2p = ctx.enter_context(tc.tile_pool(name="h2p", bufs=2))
         xtp = ctx.enter_context(tc.psum_pool(name="xtp", bufs=3))
         m1p = ctx.enter_context(tc.psum_pool(name="m1p", bufs=2))
         m2p = ctx.enter_context(tc.psum_pool(name="m2p", bufs=2))
@@ -155,7 +156,7 @@ def tile_linear_pa_t_kernel(tc, x, w0, core1, core2, out):
 
         def stage1_fold8to4(k):
             j, h = divmod(k, 2)
-            if h == 0:
+            if j not in h1s:
                 h1s[j] = ep.tile([P, 2, 4, QUAD * Q], F32, name="h1", tag="h1")
             nc.gpsimd.tensor_tensor(
                 out=h1s[j][:, h, :, :].rearrange("p r c -> p (r c)"),
@@ -176,15 +177,15 @@ def tile_linear_pa_t_kernel(tc, x, w0, core1, core2, out):
 
         def stage1_fold2to1(j):
             w1 = ep.tile([P, 2, QUAD * Q], F32, name="w1", tag="w1")
-            nc.vector.tensor_tensor(
+            nc.gpsimd.tensor_tensor(
                 out=w1[:], in0=h2s[j][:, :, 0, :], in1=h2s[j][:, :, 1, :], op=ADD
             )
             w1s[j] = w1
 
         def stage2_mul(k):
             b, i = divmod(k, BATCH // QUAD)
-            if i == 0:
-                p2s[b] = ep.tile([P, Q, BATCH, R], F32, name="p2", tag="p2")
+            if b not in p2s:
+                p2s[b] = p2p.tile([P, Q, BATCH, R], F32, name="p2", tag="p2")
             nc.vector.tensor_tensor(
                 out=p2s[b][:, :, QUAD * i : QUAD * i + QUAD, :].rearrange("p q a r -> p a q r"),
                 in0=m2s[k][:].rearrange("p a (q r) -> p a q r", r=R),
@@ -228,24 +229,24 @@ def tile_linear_pa_t_kernel(tc, x, w0, core1, core2, out):
                 stage1_fold2to1(s - 2)
             if inside(s - 1):
                 stage1_fold4to2(s - 1)
-            if inside(s - 6) and (s - 6) % 2 == 0:
-                finish_batch((s - 6) // 2)
             if inside(s + 3):
                 for h in range(3):
                     transpose_pair(s + 3, h)
                     if h < 2 and FIRST_REGROUPED <= s + 4 < NB:
                         regroup_quad(2 * (s + 4) + h)
+            if inside(s - 6) and (s - 6) % 2 == 0:
+                finish_batch((s - 6) // 2)
             if inside(s - 4):
                 b, part = divmod(s - 4, 2)
                 sum_batch(b, part * (Q // 2), (part + 1) * (Q // 2))
             if inside(s + 3):
                 transpose_pair(s + 3, 3)
             if inside(s):
-                for k in (2 * s, 2 * s + 1):
+                for k in (2 * s + 1, 2 * s):
                     stage1_mul(k)
                     stage1_fold8to4(k)
             if inside(s - 2):
-                for k in (2 * s - 4, 2 * s - 3):
+                for k in (2 * s - 3, 2 * s - 4):
                     stage2_mul(k)
             if inside(s + 1):
                 for k in (2 * s + 2, 2 * s + 3):

@@ -229,13 +229,18 @@ def tile_linear_pa_t_kernel(tc, x, w0, core1, core2, out):
                 stage1_fold2to1(s - 2)
             if inside(s - 1):
                 stage1_fold4to2(s - 1)
-            if inside(s + 3):
-                for h in range(3):
-                    transpose_pair(s + 3, h)
-                    if h < 2 and FIRST_REGROUPED <= s + 4 < NB:
-                        regroup_quad(2 * (s + 4) + h)
             if inside(s - 6) and (s - 6) % 2 == 0:
                 finish_batch((s - 6) // 2)
+            if inside(s + 3):
+                transpose_pair(s + 3, 0)
+            if FIRST_REGROUPED <= s + 4 < NB:
+                regroup_quad(2 * (s + 4) + 0)
+            if inside(s + 3):
+                transpose_pair(s + 3, 1)
+            if FIRST_REGROUPED <= s + 4 < NB:
+                regroup_quad(2 * (s + 4) + 1)
+            if inside(s + 3):
+                transpose_pair(s + 3, 2)
             if inside(s - 4):
                 b, part = divmod(s - 4, 2)
                 sum_batch(b, part * (Q // 2), (part + 1) * (Q // 2))

@@ -224,40 +224,42 @@ def tile_linear_pa_t_kernel(tc, x, w0, core1, core2, out):
         def inside(j):
             return 0 <= j < NB
 
-        for s in range(-3, NB + 7):
-            if inside(s - 2):
-                stage1_fold2to1(s - 2)
-            if inside(s - 1):
-                stage1_fold4to2(s - 1)
-            if inside(s - 6) and (s - 6) % 2 == 0:
-                finish_batch((s - 6) // 2)
+        for s in range(-4, NB + 8):
+            if inside(s + 1):
+                quantise(s + 1)
             if inside(s + 3):
                 transpose_pair(s + 3, 0)
-            if FIRST_REGROUPED <= s + 4 < NB:
-                regroup_quad(2 * (s + 4) + 0)
             if inside(s + 3):
                 transpose_pair(s + 3, 1)
-            if FIRST_REGROUPED <= s + 4 < NB:
-                regroup_quad(2 * (s + 4) + 1)
-            if inside(s + 3):
-                transpose_pair(s + 3, 2)
-            if inside(s - 4):
-                b, part = divmod(s - 4, 2)
-                sum_batch(b, part * (Q // 2), (part + 1) * (Q // 2))
-            if inside(s + 3):
-                transpose_pair(s + 3, 3)
+            if inside(s - 5) and (s - 5) % 2 == 1:
+                finish_batch((s - 5) // 2)
             if inside(s):
                 for k in (2 * s + 1, 2 * s):
                     stage1_mul(k)
-                    stage1_fold8to4(k)
-            if inside(s - 2):
-                for k in (2 * s - 3, 2 * s - 4):
-                    stage2_mul(k)
             if inside(s + 1):
                 for k in (2 * s + 2, 2 * s + 3):
                     mx_quad(k, 0, m1p, m1s)
             if inside(s - 1):
                 for k in (2 * s - 2, 2 * s - 1):
                     mx_quad(k, 1, m2p, m2s)
-            if inside(s + 2):
-                quantise(s + 2)
+            if FIRST_REGROUPED <= s + 4 < NB:
+                regroup_quad(2 * s + 8)
+            if inside(s + 3):
+                transpose_pair(s + 3, 2)
+            if inside(s + 3):
+                transpose_pair(s + 3, 3)
+            if inside(s - 4):
+                b, part = divmod(s - 4, 2)
+                sum_batch(b, part * (Q // 2), (part + 1) * (Q // 2))
+            if FIRST_REGROUPED <= s + 4 < NB:
+                regroup_quad(2 * s + 9)
+            if inside(s - 2):
+                stage1_fold2to1(s - 2)
+            if inside(s - 1):
+                stage1_fold4to2(s - 1)
+            if inside(s):
+                for k in (2 * s + 1, 2 * s):
+                    stage1_fold8to4(k)
+            if inside(s - 2):
+                for k in (2 * s - 3, 2 * s - 4):
+                    stage2_mul(k)

@@ -239,9 +239,6 @@ def tile_linear_pa_t_kernel(tc, x, w0, core1, core2, out):
             if inside(s + 1):
                 for k in (2 * s + 2, 2 * s + 3):
                     mx_quad(k, 0, m1p, m1s)
-            if inside(s - 1):
-                for k in (2 * s - 2, 2 * s - 1):
-                    mx_quad(k, 1, m2p, m2s)
             if FIRST_REGROUPED <= s + 4 < NB:
                 regroup_quad(2 * s + 8)
             if inside(s + 3):
@@ -251,6 +248,9 @@ def tile_linear_pa_t_kernel(tc, x, w0, core1, core2, out):
             if inside(s - 4):
                 b, part = divmod(s - 4, 2)
                 sum_batch(b, part * (Q // 2), (part + 1) * (Q // 2))
+            if inside(s - 1):
+                for k in (2 * s - 2, 2 * s - 1):
+                    mx_quad(k, 1, m2p, m2s)
             if FIRST_REGROUPED <= s + 4 < NB:
                 regroup_quad(2 * s + 9)
             if inside(s - 2):

@@ -39,7 +39,7 @@ def tile_linear_pa_t_kernel(tc, x, w0, core1, core2, out):
         xin = ctx.enter_context(tc.tile_pool(name="xin", bufs=1))
         gp = ctx.enter_context(tc.tile_pool(name="gp", bufs=3))
         xpp = ctx.enter_context(tc.tile_pool(name="xpp", bufs=4))
-        cp = ctx.enter_context(tc.tile_pool(name="cp", bufs=5))
+        cp = ctx.enter_context(tc.tile_pool(name="cp", bufs=4))
         p1p = ctx.enter_context(tc.tile_pool(name="p1p", bufs=4))
         ep = ctx.enter_context(tc.tile_pool(name="ep", bufs=3))
         p2p = ctx.enter_context(tc.tile_pool(name="p2p", bufs=2))
@@ -64,6 +64,9 @@ def tile_linear_pa_t_kernel(tc, x, w0, core1, core2, out):
 
         ident = const.tile([P, P], F32, name="ident")
         make_identity(nc, ident[:])
+        swap = const.tile([P, P], F32, name="swap")
+        nc.gpsimd.tensor_copy(out=swap[:, 0 : P // 2], in_=ident[:, P // 2 : P])
+        nc.gpsimd.tensor_copy(out=swap[:, P // 2 : P], in_=ident[:, 0 : P // 2])
 
         cg = const.tile([P, 2 * P, 4], BF16, name="cg", align_bytes=64)
         nc.vector.tensor_copy(
@@ -185,9 +188,14 @@ def tile_linear_pa_t_kernel(tc, x, w0, core1, core2, out):
         def stage2_mul(k):
             b, i = divmod(k, BATCH // QUAD)
             if b not in p2s:
-                p2s[b] = p2p.tile([P, Q, BATCH, R], F32, name="p2", tag="p2")
+                shape = [P, Q, BATCH, R] if b < NO - 1 else [P, 2, Q, OCT, R]
+                p2s[b] = p2p.tile(shape, F32, name="p2", tag="p2")
+            if b < NO - 1:
+                dst = p2s[b][:, :, QUAD * i : QUAD * i + QUAD, :]
+            else:
+                dst = p2s[b][:, i // 2, :, QUAD * (i % 2) : QUAD * (i % 2) + QUAD, :]
             nc.vector.tensor_tensor(
-                out=p2s[b][:, :, QUAD * i : QUAD * i + QUAD, :].rearrange("p q a r -> p a q r"),
+                out=dst.rearrange("p q a r -> p a q r"),
                 in0=m2s[k][:].rearrange("p a (q r) -> p a q r", r=R),
                 in1=w1s[k // 2][:, k % 2, :]
                 .rearrange("p (a q) -> p a q", q=Q)
@@ -198,11 +206,11 @@ def tile_linear_pa_t_kernel(tc, x, w0, core1, core2, out):
 
         def sum_batch(b, q0, q1):
             if q0 == 0:
-                obank[b] = op.tile([P, 2, P], F32, name="o", tag="o")
+                obank[b] = op.tile([P, P], F32, name="o", tag="o")
             o = obank[b]
             for q in range(q0, q1):
                 nc.tensor.matmul(
-                    out=o[:, 0, :],
+                    out=o[:],
                     lhsT=p2s[b][:, q, :, :].rearrange("p a r -> p (a r)"),
                     rhs=ident[:],
                     start=(q == 0),
@@ -211,28 +219,61 @@ def tile_linear_pa_t_kernel(tc, x, w0, core1, core2, out):
                 )
             if q1 == Q:
                 oTs = ep.tile([P, P], F32, name="oTs", tag="oTs")
-                nc.scalar.copy(out=oTs[:], in_=o[:, 0, :])
+                nc.scalar.copy(out=oTs[:], in_=o[:])
                 oTss[b] = oTs
 
+        def sum_step(j):
+            o = xtp.tile([P, P], F32, name="xt", tag="xt")
+            for i in range(Q // 2):
+                nc.tensor.matmul(
+                    out=o[:],
+                    lhsT=p2s[NO - 1][:, j % 2, 2 * i : 2 * i + 2, :, :].rearrange("p h a r -> p (h a r)"),
+                    rhs=ident[:],
+                    start=(i == 0),
+                    stop=(i == Q // 2 - 1),
+                    is_transpose=True,
+                )
+            oTs = ep.tile([P, P], F32, name="oTs", tag="oTs")
+            nc.scalar.copy(out=oTs[:], in_=o[:])
+            oTss[j, "step"] = oTs
+
+        def finish_step(j):
+            xt = xtp.tile([P, P], F32, name="xt", tag="xt")
+            for i, perm in enumerate((ident, swap)):
+                nc.tensor.matmul(
+                    out=xt[:],
+                    lhsT=oTss[j, "step"][:],
+                    rhs=perm[:],
+                    start=(i == 0),
+                    stop=(i == 1),
+                    is_transpose=True,
+                )
+            dst = out_sb[:, OCT * j : OCT * j + OCT, :]
+            nc.scalar.copy(out=dst.rearrange("p a r -> p (a r)"), in_=xt[:, 0 : OCT * R])
+            nc.sync.dma_start(out=ov[:, OCT * j : OCT * j + OCT, :], in_=dst)
+
         def finish_batch(b):
-            o = obank[b]
-            nc.tensor.transpose(o[:, 1, :], oTss[b][:], ident[:])
+            xt = xtp.tile([P, 2, 2, P], F32, name="xt", tag="xt")
+            nc.tensor.transpose(xt[:, 0, 0, :], oTss[b][:], ident[:])
             dst = out_sb[:, BATCH * b : BATCH * b + BATCH, :]
-            nc.scalar.copy(out=dst.rearrange("p a r -> p (a r)"), in_=o[:, 1, :])
+            nc.scalar.copy(out=dst.rearrange("p a r -> p (a r)"), in_=xt[:, 0, 0, :])
             nc.sync.dma_start(out=ov[:, BATCH * b : BATCH * b + BATCH, :], in_=dst)
 
         def inside(j):
             return 0 <= j < NB
 
-        for s in range(-4, NB + 8):
+        for s in range(-4, NB + 10):
             if inside(s + 1):
                 quantise(s + 1)
+            if inside(s - 6):
+                if s - 6 >= NB - 2:
+                    finish_step(s - 6)
+                elif (s - 6) % 2 == 1:
+                    finish_batch((s - 6) // 2)
             if inside(s + 3):
                 transpose_pair(s + 3, 0)
             if inside(s + 3):
                 transpose_pair(s + 3, 1)
-            if inside(s - 5) and (s - 5) % 2 == 1:
-                finish_batch((s - 5) // 2)
             if inside(s):
                 for k in (2 * s + 1, 2 * s):
                     stage1_mul(k)
@@ -246,8 +287,11 @@ def tile_linear_pa_t_kernel(tc, x, w0, core1, core2, out):
             if inside(s + 3):
                 transpose_pair(s + 3, 3)
             if inside(s - 4):
-                b, part = divmod(s - 4, 2)
-                sum_batch(b, part * (Q // 2), (part + 1) * (Q // 2))
+                if s - 4 >= NB - 2:
+                    sum_step(s - 4)
+                else:
+                    b, part = divmod(s - 4, 2)
+                    sum_batch(b, part * (Q // 2), (part + 1) * (Q // 2))
             if inside(s - 1):
                 for k in (2 * s - 2, 2 * s - 1):
                     mx_quad(k, 1, m2p, m2s)

from contextlib import ExitStack

import concourse.mybir as mybir
from concourse.masks import make_identity

F32 = mybir.dt.float32
BF16 = mybir.dt.bfloat16
U32 = mybir.dt.uint32
U8 = mybir.dt.uint8
FP8X4 = mybir.dt.float8_e4m3fn_x4
MULT = mybir.AluOpType.mult
ADD = mybir.AluOpType.add

P = 128
TOKENS = 4 * 4096
D = 512
R = 8
Q = 16
TILES = TOKENS // P
QUAD = 4
NQ = TILES // QUAD
OCT = 8
NB = TILES // OCT
BATCH = 16
NO = TILES // BATCH
FIRST_REGROUPED = 4

FLOPS = 2 * TOKENS * D * (R * Q + Q * R) + 2 * TOKENS * (R * Q + Q * R)


def tile_linear_pa_t_kernel(tc, x, w0, core1, core2, out):
    nc = tc.nc
    xv = x.flatten_outer_dims().rearrange("(p t) d -> p t d", t=TILES)
    w0v = w0.flatten_outer_dims().rearrange("(p t) r -> p t r", t=TILES)
    ov = out.flatten_outer_dims().rearrange("(p t) r -> p t r", t=TILES)

    with ExitStack() as ctx:
        const = ctx.enter_context(tc.tile_pool(name="const", bufs=1))
        xin = ctx.enter_context(tc.tile_pool(name="xin", bufs=1))
        gp = ctx.enter_context(tc.tile_pool(name="gp", bufs=3))
        xpp = ctx.enter_context(tc.tile_pool(name="xpp", bufs=4))
        cp = ctx.enter_context(tc.tile_pool(name="cp", bufs=4))
        p1p = ctx.enter_context(tc.tile_pool(name="p1p", bufs=4))
        ep = ctx.enter_context(tc.tile_pool(name="ep", bufs=3))
        p2p = ctx.enter_context(tc.tile_pool(name="p2p", bufs=2))
        h2p = ctx.enter_context(tc.tile_pool(name="h2p", bufs=2))
        xtp = ctx.enter_context(tc.psum_pool(name="xtp", bufs=3))
        m1p = ctx.enter_context(tc.psum_pool(name="m1p", bufs=2))
        m2p = ctx.enter_context(tc.psum_pool(name="m2p", bufs=2))
        op = ctx.enter_context(tc.psum_pool(name="op", bufs=1))
        ctx.enter_context(tc.manual_schedule())

        c1raw = const.tile([P, R, 4 * Q], BF16, name="c1raw")
        c2raw = const.tile([P, Q, 4 * R], BF16, name="c2raw")
        nc.scalar.dma_start(out=c1raw[:], in_=core1.rearrange("r (p e) q -> p r (e q)", e=4))
        nc.scalar.dma_start(out=c2raw[:], in_=core2.rearrange("q (p e) r -> p q (e r)", e=4))
        w0_sb = const.tile([P, TILES, R], BF16, name="w0_sb")
        nc.scalar.dma_start(out=w0_sb[:], in_=w0v)
        xq = []
        for i in range(NQ):
            xt_in = xin.tile([P, QUAD, D], BF16, name="x%d" % i)
            nc.sync.dma_start(out=xt_in[:], in_=xv[:, QUAD * i : QUAD * i + QUAD, :])
            xq.append(xt_in)

        ident = const.tile([P, P], F32, name="ident")
        make_identity(nc, ident[:])
        swap = const.tile([P, P], F32, name="swap")
        nc.gpsimd.tensor_copy(out=swap[:, 0 : P // 2], in_=ident[:, P // 2 : P])
        nc.gpsimd.tensor_copy(out=swap[:, P // 2 : P], in_=ident[:, 0 : P // 2])

        cg = const.tile([P, 2 * P, 4], BF16, name="cg", align_bytes=64)
        nc.vector.tensor_copy(
            out=cg[:, 0:P, :].rearrange("p (r q) e -> p r q e", q=Q),
            in_=c1raw[:].rearrange("p r (e q) -> p r q e", e=4),
        )
        nc.vector.tensor_copy(
            out=cg[:, P : 2 * P, :].rearrange("p (q r) e -> p q r e", r=R),
            in_=c2raw[:].rearrange("p q (e r) -> p q r e", e=4),
        )
        cc = const.tile([P, 2 * P], U32, name="cc", align_bytes=64)
        cs = const.tile([P, 2 * P], U8, name="cs", align_bytes=64)
        nc.vector.quantize_mx(
            out=cc[:].bitcast(FP8X4), scales=cs[:], in_=cg[:].rearrange("p c t -> p (c t)")
        )

        out_sb = const.tile([P, TILES, R], F32, name="out_sb")

        gs = {}
        xps = {}
        cods = {}
        m1s = {}
        m2s = {}
        p1s = {}
        h1s = {}
        h2s = {}
        w1s = {}
        p2s = {}
        obank = {}
        oTss = {}

        def regroup_quad(i):
            xp = xpp.tile([P, 2, 2, P], F32, name="xp", tag="xp")
            x32 = xq[i][:].bitcast(F32)
            nc.scalar.copy(out=xp[:], in_=x32[:, 0:QUAD:2, :].rearrange("p a (k u) -> p a u k", u=2))
            xps[i] = xp

        def transpose_pair(j, h):
            if h == 0:
                gs[j] = gp.tile([P, OCT, P, 4], BF16, name="g", tag="g", align_bytes=64)
            x32 = xq[2 * j + h // 2][:].bitcast(F32)
            xt = xtp.tile([P, 2, 2, P], F32, name="xt", tag="xt")
            for a in range(2):
                for u in range(2):
                    if a == 0 and j >= FIRST_REGROUPED:
                        src = xps[2 * j + h // 2][:, h % 2, u, :]
                    else:
                        src = x32[:, 2 * (h % 2) + a, u : 2 * P : 2]
                    nc.tensor.transpose(xt[:, a, u, :], src, ident[:])
            nc.scalar.copy(
                out=gs[j][:].bitcast(F32)[:, 2 * h : 2 * h + 2, :, :],
                in_=xt[:].rearrange("p a u k -> p a k u"),
            )

        def quantise(j):
            cod = cp.tile([P, OCT * P], U32, name="cod", tag="cod", align_bytes=64)
            scl = cp.tile([P, OCT * P], U8, name="scl", tag="scl", align_bytes=64)
            nc.vector.quantize_mx(
                out=cod[:].bitcast(FP8X4),
                scales=scl[:],
                in_=gs[j][:].rearrange("p a k t -> p (a k t)"),
            )
            cods[j] = (cod, scl)

        def mx_quad(k, half, pool, store):
            cod, scl = cods[k // 2]
            m = pool.tile([P, QUAD, P], F32, name="m%d" % half, tag="m%d" % half)
            for a in range(QUAD):
                c0 = (QUAD * (k % 2) + a) * P
                nc.tensor.matmul_mx(
                    out=m[:, a, :],
                    lhsT=cod[:, c0 : c0 + P].bitcast(FP8X4),
                    lhsT_scale=scl[:, c0 : c0 + P],
                    rhs=cc[:, half * P : (half + 1) * P].bitcast(FP8X4),
                    rhs_scale=cs[:, half * P : (half + 1) * P],
                    start=True,
                    stop=True,
                )
            store[k] = m

        def stage1_mul(k):
            p1 = p1p.tile([P, R, QUAD, Q], F32, name="p1", tag="p1")
            nc.vector.tensor_tensor(
                out=p1[:].rearrange("p r a q -> p a r q"),
                in0=m1s[k][:].rearrange("p a (r q) -> p a r q", q=Q),
                in1=w0_sb[:, QUAD * k : QUAD * k + QUAD, :].unsqueeze(3).to_broadcast([P, QUAD, R, Q]),
                op=MULT,
            )
            p1s[k] = p1

        def stage1_fold8to4(k):
            j, h = divmod(k, 2)
            if j not in h1s:
                h1s[j] = ep.tile([P, 2, 4, QUAD * Q], F32, name="h1", tag="h1")
            nc.gpsimd.tensor_tensor(
                out=h1s[j][:, h, :, :].rearrange("p r c -> p (r c)"),
                in0=p1s[k][:, 0:4, :, :].rearrange("p r a q -> p (r a q)"),
                in1=p1s[k][:, 4:8, :, :].rearrange("p r a q -> p (r a q)"),
                op=ADD,
            )

        def stage1_fold4to2(j):
            h2 = h2p.tile([P, 2, 2, QUAD * Q], F32, name="h2", tag="h2")
            nc.gpsimd.tensor_tensor(
                out=h2[:].rearrange("p h r c -> p h (r c)"),
                in0=h1s[j][:, :, 0:2, :].rearrange("p h r c -> p h (r c)"),
                in1=h1s[j][:, :, 2:4, :].rearrange("p h r c -> p h (r c)"),
                op=ADD,
            )
            h2s[j] = h2

        def stage1_fold2to1(j):
            w1 = ep.tile([P, 2, QUAD * Q], F32, name="w1", tag="w1")
            nc.gpsimd.tensor_tensor(
                out=w1[:], in0=h2s[j][:, :, 0, :], in1=h2s[j][:, :, 1, :], op=ADD
            )
            w1s[j] = w1

        def stage2_mul(k):
            b, i = divmod(k, BATCH // QUAD)
            if b not in p2s:
                shape = [P, Q, BATCH, R] if b < NO - 1 else [P, 2, Q, OCT, R]
                p2s[b] = p2p.tile(shape, F32, name="p2", tag="p2")
            if b < NO - 1:
                dst = p2s[b][:, :, QUAD * i : QUAD * i + QUAD, :]
            else:
                dst = p2s[b][:, i // 2, :, QUAD * (i % 2) : QUAD * (i % 2) + QUAD, :]
            nc.vector.tensor_tensor(
                out=dst.rearrange("p q a r -> p a q r"),
                in0=m2s[k][:].rearrange("p a (q r) -> p a q r", r=R),
                in1=w1s[k // 2][:, k % 2, :]
                .rearrange("p (a q) -> p a q", q=Q)
                .unsqueeze(3)
                .to_broadcast([P, QUAD, Q, R]),
                op=MULT,
            )

        def sum_batch(b, q0, q1):
            if q0 == 0:
                obank[b] = op.tile([P, P], F32, name="o", tag="o")
            o = obank[b]
            for q in range(q0, q1):
                nc.tensor.matmul(
                    out=o[:],
                    lhsT=p2s[b][:, q, :, :].rearrange("p a r -> p (a r)"),
                    rhs=ident[:],
                    start=(q == 0),
                    stop=(q == Q - 1),
                    is_transpose=True,
                )
            if q1 == Q:
                oTs = ep.tile([P, P], F32, name="oTs", tag="oTs")
                nc.scalar.copy(out=oTs[:], in_=o[:])
                oTss[b] = oTs

        def sum_step(j):
            o = xtp.tile([P, P], F32, name="xt", tag="xt")
            for i in range(Q // 2):
                nc.tensor.matmul(
                    out=o[:],
                    lhsT=p2s[NO - 1][:, j % 2, 2 * i : 2 * i + 2, :, :].rearrange("p h a r -> p (h a r)"),
                    rhs=ident[:],
                    start=(i == 0),
                    stop=(i == Q // 2 - 1),
                    is_transpose=True,
                )
            oTs = ep.tile([P, P], F32, name="oTs", tag="oTs")
            nc.scalar.copy(out=oTs[:], in_=o[:])
            oTss[j, "step"] = oTs

        def finish_step(j):
            xt = xtp.tile([P, P], F32, name="xt", tag="xt")
            for i, perm in enumerate((ident, swap)):
                nc.tensor.matmul(
                    out=xt[:],
                    lhsT=oTss[j, "step"][:],
                    rhs=perm[:],
                    start=(i == 0),
                    stop=(i == 1),
                    is_transpose=True,
                )
            dst = out_sb[:, OCT * j : OCT * j + OCT, :]
            nc.scalar.copy(out=dst.rearrange("p a r -> p (a r)"), in_=xt[:, 0 : OCT * R])
            nc.sync.dma_start(out=ov[:, OCT * j : OCT * j + OCT, :], in_=dst)

        def finish_batch(b):
            xt = xtp.tile([P, 2, 2, P], F32, name="xt", tag="xt")
            nc.tensor.transpose(xt[:, 0, 0, :], oTss[b][:], ident[:])
            dst = out_sb[:, BATCH * b : BATCH * b + BATCH, :]
            nc.scalar.copy(out=dst.rearrange("p a r -> p (a r)"), in_=xt[:, 0, 0, :])
            nc.sync.dma_start(out=ov[:, BATCH * b : BATCH * b + BATCH, :], in_=dst)

        def inside(j):
            return 0 <= j < NB

        for s in range(-4, NB + 10):
            if inside(s + 1):
                quantise(s + 1)
            if inside(s - 6):
                if s - 6 >= NB - 2:
                    finish_step(s - 6)
                elif (s - 6) % 2 == 1:
                    finish_batch((s - 6) // 2)
            if inside(s + 3):
                transpose_pair(s + 3, 0)
            if inside(s + 3):
                transpose_pair(s + 3, 1)
            if inside(s):
                for k in (2 * s + 1, 2 * s):
                    stage1_mul(k)
            if inside(s + 1):
                for k in (2 * s + 2, 2 * s + 3):
                    mx_quad(k, 0, m1p, m1s)
            if FIRST_REGROUPED <= s + 4 < NB:
                regroup_quad(2 * s + 8)
            if inside(s + 3):
                transpose_pair(s + 3, 2)
            if inside(s + 3):
                transpose_pair(s + 3, 3)
            if inside(s - 4):
                if s - 4 >= NB - 2:
                    sum_step(s - 4)
                else:
                    b, part = divmod(s - 4, 2)
                    sum_batch(b, part * (Q // 2), (part + 1) * (Q // 2))
            if inside(s - 1):
                for k in (2 * s - 2, 2 * s - 1):
                    mx_quad(k, 1, m2p, m2s)
            if FIRST_REGROUPED <= s + 4 < NB:
                regroup_quad(2 * s + 9)
            if inside(s - 2):
                stage1_fold2to1(s - 2)
            if inside(s - 1):
                stage1_fold4to2(s - 1)
            if inside(s):
                for k in (2 * s + 1, 2 * s):
                    stage1_fold8to4(k)
            if inside(s - 2):
                for k in (2 * s - 3, 2 * s - 4):
                    stage2_mul(k)
